import numpy as np
import ml_dtypes


def mxq(x, axis, fmt="e4m3"):
    dtype, down = {"e4m3": (ml_dtypes.float8_e4m3fn, 7), "e5m2": (ml_dtypes.float8_e5m2, 14)}[fmt]
    v = np.moveaxis(np.asarray(x, np.float32).astype(ml_dtypes.bfloat16).astype(np.float64), axis, -1)
    blocks = v.reshape(v.shape[:-1] + (-1, 32))
    amax = np.abs(blocks).max(-1, keepdims=True)
    byte = np.maximum(np.where(amax > 0, np.frexp(amax)[1] - 1 + 127, 0) - down, 1)
    scale = np.exp2(byte - 127.0)
    codes = (blocks / scale).astype(np.float32).astype(dtype).astype(np.float64)
    return np.moveaxis((codes * scale).reshape(v.shape), -1, axis)


WIDE = False


def mx_kscale(k):
    if not WIDE:
        return np.ones(k)
    levels = np.array([30, -30])
    if k % 512:
        return np.exp2(np.random.permutation(np.resize(levels, k // 32))).repeat(32)
    a = np.empty((k // 512, 16))
    for p in range(k // 512):
        a[p, :8] = np.random.permutation(np.resize(levels, 8))
        for g in range(8):
            far = levels[np.abs(levels - a[p, g]) >= 10]
            a[p, g + 8] = far[np.random.randint(len(far))]
    return np.exp2(a.ravel()).repeat(32)


BF16 = ml_dtypes.bfloat16


def bf(x):
    return np.asarray(x, np.float32).astype(BF16)


def f64(x):
    return np.asarray(x).astype(np.float64)


B, S, D, NH, NKV, HD = 2, 256, 2048, 16, 4, 128
EPS = 1e-6
QS = NH * HD
KS = NKV * HD
E = QS + KS + KS
HP = HD // 2


def rmsnorm(v, w):
    ms = np.mean(np.square(v), axis=-1, keepdims=True)
    return v * (1.0 / np.sqrt(ms + EPS)) * w


def apply_rotary_emb(v, fc):
    vs = v.reshape(*v.shape[:-1], HP, 2)
    f = fc[None, :, None, :, :]
    vr, vi = vs[..., 0], vs[..., 1]
    fr, fi = f[..., 0], f[..., 1]
    return np.stack([vr * fr - vi * fi, vi * fr + vr * fi], axis=-1).reshape(v.shape)


def setup_inputs():
    s = mx_kscale(D)
    return {"x": bf(np.random.standard_normal((B, S, D)) * s),
            "freqs_cis": bf(np.random.standard_normal((S, HP, 2))),
            "wqkv": bf(np.random.standard_normal((E, D)) / np.sqrt(D) / s[None, :]),
            "q_norm_w": bf(1.0 + 0.1 * np.random.standard_normal(HD)),
            "k_norm_w": bf(1.0 + 0.1 * np.random.standard_normal(HD))}


def reference(x, freqs_cis, wqkv, q_norm_w, k_norm_w):
    fc = f64(freqs_cis)
    qkv = mxq(f64(x), 2, "e5m2") @ mxq(f64(wqkv), 1, "e5m2").T
    q = qkv[..., :QS].reshape(B, S, NH, HD)
    k = qkv[..., QS:QS + KS].reshape(B, S, NKV, HD)
    v = qkv[..., QS + KS:].reshape(B, S, NKV, HD)
    q = rmsnorm(q, f64(q_norm_w))
    k = rmsnorm(k, f64(k_norm_w))
    q_rot = apply_rotary_emb(q, fc)
    k_rot = apply_rotary_emb(k, fc)
    return q_rot, k_rot, v

@@ -1,0 +1,236 @@
+from contextlib import ExitStack
+
+import concourse.mybir as mybir
+from concourse.masks import make_identity
+
+F32 = mybir.dt.float32
+BF16 = mybir.dt.bfloat16
+U32 = mybir.dt.uint32
+U8 = mybir.dt.uint8
+E5X4 = mybir.dt.float8_e5m2_x4
+ACT = mybir.ActivationFunctionType
+ALU = mybir.AluOpType
+
+P = 128
+TOKENS = 512
+D = 2048
+E = 3072
+HD = 128
+EPS = 1e-6
+NRUN = 14
+LAG = 4
+
+FLOPS = 2 * TOKENS * E * D
+
+
+def pairs(ap):
+    return ap.rearrange("p (j e) -> p j e", e=2)
+
+
+def tile_attention_pa_kernel(tc, x, freqs_cis, wqkv, q_norm_w, k_norm_w, out_0, out_1, out_2):
+    nc = tc.nc
+    x_rows = x.rearrange("b s k -> (b s) k")
+    q_out = out_0.rearrange("b s h d -> (b s) (h d)")
+    k_out = out_1.rearrange("b s h d -> (b s) (h d)")
+    v_out = out_2.rearrange("b s h d -> (b s) (h d)")
+
+    with ExitStack() as ctx:
+        const = ctx.enter_context(tc.tile_pool(name="const", bufs=1))
+        keep = ctx.enter_context(tc.tile_pool(name="keep", bufs=1))
+        rawx = ctx.enter_context(tc.tile_pool(name="rawx", bufs=4))
+        raww = ctx.enter_context(tc.tile_pool(name="raww", bufs=6))
+        grp = ctx.enter_context(tc.tile_pool(name="grp", bufs=4))
+        small = ctx.enter_context(tc.tile_pool(name="small", bufs=4))
+        work = ctx.enter_context(tc.tile_pool(name="work", bufs=4))
+        tps = ctx.enter_context(tc.psum_pool(name="tps", bufs=4))
+        accs = ctx.enter_context(tc.psum_pool(name="accs", bufs=4))
+        ctx.enter_context(tc.manual_schedule())
+
+        raws = {}
+        codes = {}
+        scales = {}
+        acc_of = {}
+        rs_of = {}
+        t1_of = {}
+        t2_of = {}
+
+        def load_x(m):
+            raw = rawx.tile([P, D], BF16, name="rx")
+            nc.sync.dma_start(out=raw[:], in_=x_rows[m * P : (m + 1) * P, :])
+            raws[m] = raw
+
+        def load_w(i):
+            n, kh = divmod(i, 2)
+            raw = raww.tile([P, 4, 1024], BF16, name="rw")
+            rows = wqkv[n * 512 : (n + 1) * 512, kh * 1024 : (kh + 1) * 1024]
+            nc.sync.dma_start(out=raw[:], in_=rows.rearrange("(t p) k -> p t k", p=P))
+            raws[4 + 2 * i] = raw
+            raws[5 + 2 * i] = raw
+
+        def slab(unit, s, u):
+            if unit < 4:
+                return raws[unit][:].bitcast(F32)[:, 256 * s + u : 256 * (s + 1) : 2]
+            gl = unit % 2
+            return raws[unit][:, s, :].bitcast(F32)[:, 256 * gl + u : 256 * (gl + 1) : 2]
+
+        wrow = const.tile([P, 2 * HD], BF16, name="wrow")
+        nc.gpsimd.memset(wrow[:], 0.0)
+        freqs = const.tile([P, 2, HD], BF16, name="freqs")
+        nc.scalar.dma_start(out=freqs[:], in_=freqs_cis.rearrange("(t p) j e -> p t (j e)", p=P))
+        nc.scalar.dma_start(out=wrow[0:1, 0:HD], in_=q_norm_w.rearrange("(o d) -> o d", o=1))
+        nc.scalar.dma_start(out=wrow[0:1, HD : 2 * HD], in_=k_norm_w.rearrange("(o d) -> o d", o=1))
+        for m in range(4):
+            load_x(m)
+        for i in range(2):
+            load_w(i)
+        ident = const.tile([P, P], F32, name="ident")
+        make_identity(nc, ident[:])
+        ones = const.tile([P, P], BF16, name="ones")
+        nc.gpsimd.memset(ones[:], 1.0)
+        warm = const.tile([P, 1], F32, name="warm")
+        nc.gpsimd.memset(warm[:], 1.0)
+        warm2 = const.tile([P, 1], F32, name="warm2")
+        nc.scalar.activation(out=warm2[:], in_=warm[:], func=ACT.Abs_reciprocal_sqrt)
+        junk = const.tile([P, 4 * HD], F32, name="junk")
+        tab = const.tile([P, 2, 2, 2, HD], F32, name="tab")
+
+        def spread_gains():
+            wb = accs.tile([P, 512], F32, name="acc")
+            nc.tensor.matmul(out=wb[:, 0 : 2 * HD], lhsT=ones[:], rhs=wrow[:], start=True, stop=True)
+            return wb
+
+        def tables(wb):
+            for ws in range(2):
+                w3 = pairs(wb[:, ws * HD : (ws + 1) * HD])
+                for pt in range(2):
+                    f3 = pairs(freqs[:, pt, :])
+                    c1 = pairs(tab[:, ws, pt, 0, :])
+                    c2 = pairs(tab[:, ws, pt, 1, :])
+                    for e in range(2):
+                        nc.vector.tensor_tensor(
+                            out=c1[:, :, e : e + 1], in0=w3[:, :, e : e + 1], in1=f3[:, :, 0:1], op=ALU.mult
+                        )
+                    nc.vector.scalar_tensor_tensor(
+                        out=c2[:, :, 0:1], in0=w3[:, :, 1:2], scalar=-1.0, in1=f3[:, :, 1:2],
+                        op0=ALU.mult, op1=ALU.mult,
+                    )
+                    nc.vector.tensor_tensor(out=c2[:, :, 1:2], in0=w3[:, :, 0:1], in1=f3[:, :, 1:2], op=ALU.mult)
+
+        def transposes(unit):
+            gt = grp.tile([P, 2048], BF16, name="grouped", align_bytes=64)
+            gw = gt[:].bitcast(F32)
+            for b in range(2):
+                tp = tps.tile([P, 2, 2, P], F32, name="tp")
+                for sl in range(2):
+                    for u in range(2):
+                        nc.tensor.transpose(tp[:, sl, u, :], slab(unit, 2 * b + sl, u), ident[:])
+                nc.scalar.copy(
+                    out=gw[:, 512 * b : 512 * (b + 1)].rearrange("p (s r u) -> p s r u", s=2, u=2),
+                    in_=tp[:].rearrange("p s u r -> p s r u"),
+                )
+            return gt
+
+        def quantize(unit, gt):
+            cd = keep.tile([P, 512], U32, name="cd%d" % unit, align_bytes=64)
+            sc = keep.tile([P, 512], U8, name="sc%d" % unit, align_bytes=64)
+            nc.vector.quantize_mx(out=cd[:].bitcast(E5X4), scales=sc[:], in_=gt[:])
+            codes[unit] = cd
+            scales[unit] = sc
+
+        def mx(j):
+            n, m = divmod(j, 4)
+            acc = accs.tile([P, 512], F32, name="acc")
+            for g in range(4):
+                cols = slice(g * P, (g + 1) * P)
+                nc.tensor.matmul_mx(
+                    out=acc[:],
+                    lhsT=codes[m][:, cols].bitcast(E5X4),
+                    lhsT_scale=scales[m][:, cols],
+                    rhs=codes[4 + 4 * n + g][:].bitcast(E5X4),
+                    rhs_scale=scales[4 + 4 * n + g][:],
+                    start=(g == 0),
+                    stop=(g == 3),
+                )
+            acc_of[j] = acc
+
+        def stats(j):
+            acc = acc_of[j]
+            ss = small.tile([P, 4], F32, name="ss")
+            for h in range(4):
+                sl = slice(h * HD, (h + 1) * HD)
+                nc.scalar.activation(out=junk[:, sl], in_=acc[:, sl], func=ACT.Square, accum_out=ss[:, h : h + 1])
+            rs = small.tile([P, 4], F32, name="rs")
+            nc.scalar.activation(out=rs[:], in_=ss[:], func=ACT.Abs_reciprocal_sqrt, scale=1.0 / HD, bias=EPS)
+            rs_of[j] = rs
+
+        def rotate(j):
+            n, m = divmod(j, 4)
+            ws = 0 if n < 4 else 1
+            pt = m % 2
+            acc = acc_of[j]
+            rs = rs_of[j]
+            t1 = work.tile([P, 512], F32, name="t1")
+            t2 = work.tile([P, 512], F32, name="t2")
+            for h in range(4):
+                sl = slice(h * HD, (h + 1) * HD)
+                nc.vector.scalar_tensor_tensor(
+                    out=t1[:, sl], in0=acc[:, sl], scalar=rs[:, h : h + 1], in1=tab[:, ws, pt, 0, :],
+                    op0=ALU.mult, op1=ALU.mult,
+                )
+            for h in range(4):
+                sl = slice(h * HD, (h + 1) * HD)
+                nc.vector.scalar_tensor_tensor(
+                    out=pairs(t2[:, sl]), in0=pairs(acc[:, sl])[:, :, ::-1], scalar=rs[:, h : h + 1],
+                    in1=pairs(tab[:, ws, pt, 1, :]), op0=ALU.mult, op1=ALU.mult,
+                )
+            t1_of[j] = t1
+            t2_of[j] = t2
+
+        def finish(j):
+            n, m = divmod(j, 4)
+            t1 = t1_of[j]
+            rows = slice(m * P, (m + 1) * P)
+            if n < 5:
+                nc.gpsimd.tensor_tensor(out=t1[:], in0=t1[:], in1=t2_of[j][:], op=ALU.add)
+            if n < 4:
+                dest = q_out[rows, n * 512 : (n + 1) * 512]
+            elif n == 4:
+                dest = k_out[rows, :]
+            else:
+                dest = v_out[rows, :]
+            nc.sync.dma_start(out=dest, in_=t1[:])
+
+        def plain_copy(j):
+            t1 = work.tile([P, 512], F32, name="t1")
+            if j % 2 == 0:
+                nc.scalar.copy(out=t1[:], in_=acc_of[j][:])
+            else:
+                nc.vector.tensor_copy(out=t1[:], in_=acc_of[j][:])
+            t1_of[j] = t1
+
+        for r in range(NRUN + 2):
+            if r + 2 < 12:
+                load_w(r + 2)
+            grouped = []
+            if r < NRUN:
+                for unit in (2 * r, 2 * r + 1):
+                    grouped.append((unit, transposes(unit)))
+            if r == 1:
+                gains = spread_gains()
+            banks = [2 * (r - LAG), 2 * (r - LAG) + 1] if r >= LAG else []
+            for j in banks:
+                mx(j)
+            for unit, gt in grouped:
+                quantize(unit, gt)
+            if r == 1:
+                tables(gains)
+            for j in banks:
+                if j < 20:
+                    stats(j)
+                else:
+                    plain_copy(j)
+            for j in banks:
+                if j < 20:
+                    rotate(j)
+            for j in banks:
+                finish(j)

@@ -19,6 +19,7 @@ HD = 128
 EPS = 1e-6
 NRUN = 14
 LAG = 4
+WARM_START = 6
 
 FLOPS = 2 * TOKENS * E * D
 
@@ -73,6 +74,17 @@ def tile_attention_pa_kernel(tc, x, freqs_cis, wqkv, q_norm_w, k_norm_w, out_0, 
             gl = unit % 2
             return raws[unit][:, s, :].bitcast(F32)[:, 256 * gl + u : 256 * (gl + 1) : 2]
 
+        ones = const.tile([P, P], BF16, name="ones")
+        nc.vector.memset(ones[:], 1.0)
+        filler = const.tile([P, 512], BF16, name="filler")
+        nc.vector.memset(filler[:], 0.0)
+        idle_bank = accs.tile([P, 512], F32, name="acc")
+
+        def keep_warm(count):
+            for i in range(count):
+                nc.tensor.matmul(out=idle_bank[:], lhsT=ones[:], rhs=filler[:], start=True, stop=True)
+
+        keep_warm(WARM_START)
         wrow = const.tile([P, 2 * HD], BF16, name="wrow")
         nc.gpsimd.memset(wrow[:], 0.0)
         freqs = const.tile([P, 2, HD], BF16, name="freqs")
@@ -85,8 +97,6 @@ def tile_attention_pa_kernel(tc, x, freqs_cis, wqkv, q_norm_w, k_norm_w, out_0, 
             load_w(i)
         ident = const.tile([P, P], F32, name="ident")
         make_identity(nc, ident[:])
-        ones = const.tile([P, P], BF16, name="ones")
-        nc.gpsimd.memset(ones[:], 1.0)
         warm = const.tile([P, 1], F32, name="warm")
         nc.gpsimd.memset(warm[:], 1.0)
         warm2 = const.tile([P, 1], F32, name="warm2")
@@ -215,6 +225,8 @@ def tile_attention_pa_kernel(tc, x, freqs_cis, wqkv, q_norm_w, k_norm_w, out_0, 
             if r < NRUN:
                 for unit in (2 * r, 2 * r + 1):
                     grouped.append((unit, transposes(unit)))
+                    if r <= LAG:
+                        keep_warm(1)
             if r == 1:
                 gains = spread_gains()
             banks = [2 * (r - LAG), 2 * (r - LAG) + 1] if r >= LAG else []

@@ -19,7 +19,7 @@ HD = 128
 EPS = 1e-6
 NRUN = 14
 LAG = 4
-WARM_START = 6
+AHEAD = 8
 
 FLOPS = 2 * TOKENS * E * D
 
@@ -38,11 +38,11 @@ def tile_attention_pa_kernel(tc, x, freqs_cis, wqkv, q_norm_w, k_norm_w, out_0, 
     with ExitStack() as ctx:
         const = ctx.enter_context(tc.tile_pool(name="const", bufs=1))
         keep = ctx.enter_context(tc.tile_pool(name="keep", bufs=1))
-        rawx = ctx.enter_context(tc.tile_pool(name="rawx", bufs=4))
-        raww = ctx.enter_context(tc.tile_pool(name="raww", bufs=6))
+        rawp = ctx.enter_context(tc.tile_pool(name="rawp", bufs=12))
         grp = ctx.enter_context(tc.tile_pool(name="grp", bufs=4))
         small = ctx.enter_context(tc.tile_pool(name="small", bufs=4))
         work = ctx.enter_context(tc.tile_pool(name="work", bufs=4))
+        outp = ctx.enter_context(tc.tile_pool(name="outp", bufs=8))
         tps = ctx.enter_context(tc.psum_pool(name="tps", bufs=4))
         accs = ctx.enter_context(tc.psum_pool(name="accs", bufs=4))
         ctx.enter_context(tc.manual_schedule())
@@ -55,48 +55,28 @@ def tile_attention_pa_kernel(tc, x, freqs_cis, wqkv, q_norm_w, k_norm_w, out_0, 
         t1_of = {}
         t2_of = {}
 
-        def load_x(m):
-            raw = rawx.tile([P, D], BF16, name="rx")
-            nc.sync.dma_start(out=raw[:], in_=x_rows[m * P : (m + 1) * P, :])
-            raws[m] = raw
+        def load(unit):
+            raw = rawp.tile([P, D], BF16, name="raw")
+            rows = x_rows if unit < 4 else wqkv
+            r0 = (unit % 4 if unit < 4 else unit - 4) * P
+            nc.sync.dma_start(out=raw[:], in_=rows[r0 : r0 + P, :])
+            raws[unit] = raw
 
-        def load_w(i):
-            n, kh = divmod(i, 2)
-            raw = raww.tile([P, 4, 1024], BF16, name="rw")
-            rows = wqkv[n * 512 : (n + 1) * 512, kh * 1024 : (kh + 1) * 1024]
-            nc.sync.dma_start(out=raw[:], in_=rows.rearrange("(t p) k -> p t k", p=P))
-            raws[4 + 2 * i] = raw
-            raws[5 + 2 * i] = raw
+        def slab(unit, g, u):
+            return raws[unit][:].bitcast(F32)[:, 256 * g + u : 256 * (g + 1) : 2]
 
-        def slab(unit, s, u):
-            if unit < 4:
-                return raws[unit][:].bitcast(F32)[:, 256 * s + u : 256 * (s + 1) : 2]
-            gl = unit % 2
-            return raws[unit][:, s, :].bitcast(F32)[:, 256 * gl + u : 256 * (gl + 1) : 2]
-
-        ones = const.tile([P, P], BF16, name="ones")
-        nc.vector.memset(ones[:], 1.0)
-        filler = const.tile([P, 512], BF16, name="filler")
-        nc.vector.memset(filler[:], 0.0)
-        idle_bank = accs.tile([P, 512], F32, name="acc")
-
-        def keep_warm(count):
-            for i in range(count):
-                nc.tensor.matmul(out=idle_bank[:], lhsT=ones[:], rhs=filler[:], start=True, stop=True)
-
-        keep_warm(WARM_START)
         wrow = const.tile([P, 2 * HD], BF16, name="wrow")
         nc.gpsimd.memset(wrow[:], 0.0)
         freqs = const.tile([P, 2, HD], BF16, name="freqs")
         nc.scalar.dma_start(out=freqs[:], in_=freqs_cis.rearrange("(t p) j e -> p t (j e)", p=P))
         nc.scalar.dma_start(out=wrow[0:1, 0:HD], in_=q_norm_w.rearrange("(o d) -> o d", o=1))
         nc.scalar.dma_start(out=wrow[0:1, HD : 2 * HD], in_=k_norm_w.rearrange("(o d) -> o d", o=1))
-        for m in range(4):
-            load_x(m)
-        for i in range(2):
-            load_w(i)
+        for unit in range(AHEAD):
+            load(unit)
         ident = const.tile([P, P], F32, name="ident")
         make_identity(nc, ident[:])
+        ones = const.tile([P, P], BF16, name="ones")
+        nc.gpsimd.memset(ones[:], 1.0)
         warm = const.tile([P, 1], F32, name="warm")
         nc.gpsimd.memset(warm[:], 1.0)
         warm2 = const.tile([P, 1], F32, name="warm2")
@@ -141,23 +121,39 @@ def tile_attention_pa_kernel(tc, x, freqs_cis, wqkv, q_norm_w, k_norm_w, out_0, 
             return gt
 
         def quantize(unit, gt):
-            cd = keep.tile([P, 512], U32, name="cd%d" % unit, align_bytes=64)
-            sc = keep.tile([P, 512], U8, name="sc%d" % unit, align_bytes=64)
-            nc.vector.quantize_mx(out=cd[:].bitcast(E5X4), scales=sc[:], in_=gt[:])
-            codes[unit] = cd
-            scales[unit] = sc
+            if unit < 4:
+                cd = keep.tile([P, 4, P], U32, name="xc%d" % unit, align_bytes=64)
+                sc = keep.tile([P, 4, P], U8, name="xs%d" % unit, align_bytes=64)
+                nc.vector.quantize_mx(
+                    out=cd[:].rearrange("p g r -> p (g r)").bitcast(E5X4),
+                    scales=sc[:].rearrange("p g r -> p (g r)"),
+                    in_=gt[:],
+                )
+                codes[unit] = cd
+                scales[unit] = sc
+                return
+            n, t = divmod(unit - 4, 4)
+            if t == 0:
+                codes[4 + n] = keep.tile([P, 4, 512], U32, name="wc%d" % n, align_bytes=64)
+                scales[4 + n] = keep.tile([P, 4, 512], U8, name="ws%d" % n, align_bytes=64)
+            cols = slice(t * P, (t + 1) * P)
+            for g in range(4):
+                nc.vector.quantize_mx(
+                    out=codes[4 + n][:, g, cols].bitcast(E5X4),
+                    scales=scales[4 + n][:, g, cols],
+                    in_=gt[:, g * 512 : (g + 1) * 512],
+                )
 
         def mx(j):
             n, m = divmod(j, 4)
             acc = accs.tile([P, 512], F32, name="acc")
             for g in range(4):
-                cols = slice(g * P, (g + 1) * P)
                 nc.tensor.matmul_mx(
                     out=acc[:],
-                    lhsT=codes[m][:, cols].bitcast(E5X4),
-                    lhsT_scale=scales[m][:, cols],
-                    rhs=codes[4 + 4 * n + g][:].bitcast(E5X4),
-                    rhs_scale=scales[4 + 4 * n + g][:],
+                    lhsT=codes[m][:, g, :].bitcast(E5X4),
+                    lhsT_scale=scales[m][:, g, :],
+                    rhs=codes[4 + n][:, g, :].bitcast(E5X4),
+                    rhs_scale=scales[4 + n][:, g, :],
                     start=(g == 0),
                     stop=(g == 3),
                 )
@@ -179,7 +175,7 @@ def tile_attention_pa_kernel(tc, x, freqs_cis, wqkv, q_norm_w, k_norm_w, out_0, 
             pt = m % 2
             acc = acc_of[j]
             rs = rs_of[j]
-            t1 = work.tile([P, 512], F32, name="t1")
+            t1 = outp.tile([P, 512], F32, name="t1")
             t2 = work.tile([P, 512], F32, name="t2")
             for h in range(4):
                 sl = slice(h * HD, (h + 1) * HD)
@@ -211,7 +207,7 @@ def tile_attention_pa_kernel(tc, x, freqs_cis, wqkv, q_norm_w, k_norm_w, out_0, 
             nc.sync.dma_start(out=dest, in_=t1[:])
 
         def plain_copy(j):
-            t1 = work.tile([P, 512], F32, name="t1")
+            t1 = outp.tile([P, 512], F32, name="t1")
             if j % 2 == 0:
                 nc.scalar.copy(out=t1[:], in_=acc_of[j][:])
             else:
@@ -219,14 +215,13 @@ def tile_attention_pa_kernel(tc, x, freqs_cis, wqkv, q_norm_w, k_norm_w, out_0, 
             t1_of[j] = t1
 
         for r in range(NRUN + 2):
-            if r + 2 < 12:
-                load_w(r + 2)
+            for unit in (2 * r + AHEAD, 2 * r + AHEAD + 1):
+                if unit < 2 * NRUN:
+                    load(unit)
             grouped = []
             if r < NRUN:
                 for unit in (2 * r, 2 * r + 1):
                     grouped.append((unit, transposes(unit)))
-                    if r <= LAG:
-                        keep_warm(1)
             if r == 1:
                 gains = spread_gains()
             banks = [2 * (r - LAG), 2 * (r - LAG) + 1] if r >= LAG else []

@@ -52,18 +52,30 @@ def tile_attention_pa_kernel(tc, x, freqs_cis, wqkv, q_norm_w, k_norm_w, out_0, 
         scales = {}
         acc_of = {}
         rs_of = {}
-        t1_of = {}
-        t2_of = {}
+        pp_of = {}
+        out_of = {}
 
-        def load(unit):
-            raw = rawp.tile([P, D], BF16, name="raw")
-            rows = x_rows if unit < 4 else wqkv
-            r0 = (unit % 4 if unit < 4 else unit - 4) * P
-            nc.sync.dma_start(out=raw[:], in_=rows[r0 : r0 + P, :])
-            raws[unit] = raw
+        def load(i):
+            if i < 4:
+                raw = rawp.tile([P, D], BF16, name="raw")
+                nc.sync.dma_start(out=raw[:], in_=x_rows[i * P : (i + 1) * P, :])
+            else:
+                run, half = divmod(i - 4, 2)
+                n, kh = divmod(run, 2)
+                r0 = n * 512 + half * 256
+                raw = rawp.tile([P, 2, 1024], BF16, name="raw")
+                nc.sync.dma_start(
+                    out=raw[:],
+                    in_=wqkv[r0 : r0 + 256, kh * 1024 : (kh + 1) * 1024].rearrange("(t p) k -> p t k", p=P),
+                )
+            raws[i] = raw
 
-        def slab(unit, g, u):
-            return raws[unit][:].bitcast(F32)[:, 256 * g + u : 256 * (g + 1) : 2]
+        def slab(unit, s, u):
+            if unit < 4:
+                return raws[unit][:].bitcast(F32)[:, 256 * s + u : 256 * (s + 1) : 2]
+            gl = unit % 2
+            raw = raws[4 + 2 * (unit // 2 - 2) + s // 2]
+            return raw[:, s % 2, :].bitcast(F32)[:, 256 * gl + u : 256 * (gl + 1) : 2]
 
         wrow = const.tile([P, 2 * HD], BF16, name="wrow")
         nc.gpsimd.memset(wrow[:], 0.0)
@@ -71,8 +83,8 @@ def tile_attention_pa_kernel(tc, x, freqs_cis, wqkv, q_norm_w, k_norm_w, out_0, 
         nc.scalar.dma_start(out=freqs[:], in_=freqs_cis.rearrange("(t p) j e -> p t (j e)", p=P))
         nc.scalar.dma_start(out=wrow[0:1, 0:HD], in_=q_norm_w.rearrange("(o d) -> o d", o=1))
         nc.scalar.dma_start(out=wrow[0:1, HD : 2 * HD], in_=k_norm_w.rearrange("(o d) -> o d", o=1))
-        for unit in range(AHEAD):
-            load(unit)
+        for i in range(AHEAD):
+            load(i)
         ident = const.tile([P, P], F32, name="ident")
         make_identity(nc, ident[:])
         ones = const.tile([P, P], BF16, name="ones")
@@ -100,60 +112,40 @@ def tile_attention_pa_kernel(tc, x, freqs_cis, wqkv, q_norm_w, k_norm_w, out_0, 
                         nc.vector.tensor_tensor(
                             out=c1[:, :, e : e + 1], in0=w3[:, :, e : e + 1], in1=f3[:, :, 0:1], op=ALU.mult
                         )
+                    nc.vector.tensor_tensor(out=c2[:, :, 0:1], in0=w3[:, :, 0:1], in1=f3[:, :, 1:2], op=ALU.mult)
                     nc.vector.scalar_tensor_tensor(
-                        out=c2[:, :, 0:1], in0=w3[:, :, 1:2], scalar=-1.0, in1=f3[:, :, 1:2],
+                        out=c2[:, :, 1:2], in0=w3[:, :, 1:2], scalar=-1.0, in1=f3[:, :, 1:2],
                         op0=ALU.mult, op1=ALU.mult,
                     )
-                    nc.vector.tensor_tensor(out=c2[:, :, 1:2], in0=w3[:, :, 0:1], in1=f3[:, :, 1:2], op=ALU.mult)
 
-        def transposes(unit):
-            gt = grp.tile([P, 2048], BF16, name="grouped", align_bytes=64)
-            gw = gt[:].bitcast(F32)
-            for b in range(2):
-                tp = tps.tile([P, 2, 2, P], F32, name="tp")
-                for sl in range(2):
-                    for u in range(2):
-                        nc.tensor.transpose(tp[:, sl, u, :], slab(unit, 2 * b + sl, u), ident[:])
-                nc.scalar.copy(
-                    out=gw[:, 512 * b : 512 * (b + 1)].rearrange("p (s r u) -> p s r u", s=2, u=2),
-                    in_=tp[:].rearrange("p s u r -> p s r u"),
-                )
-            return gt
+        def transposes(unit, b, gt):
+            tp = tps.tile([P, 2, 2, P], F32, name="tp")
+            for sl in range(2):
+                for u in range(2):
+                    nc.tensor.transpose(tp[:, sl, u, :], slab(unit, 2 * b + sl, u), ident[:])
+            nc.scalar.copy(
+                out=gt[:].bitcast(F32)[:, 512 * b : 512 * (b + 1)].rearrange("p (s r u) -> p s r u", s=2, u=2),
+                in_=tp[:].rearrange("p s u r -> p s r u"),
+            )
 
         def quantize(unit, gt):
-            if unit < 4:
-                cd = keep.tile([P, 4, P], U32, name="xc%d" % unit, align_bytes=64)
-                sc = keep.tile([P, 4, P], U8, name="xs%d" % unit, align_bytes=64)
-                nc.vector.quantize_mx(
-                    out=cd[:].rearrange("p g r -> p (g r)").bitcast(E5X4),
-                    scales=sc[:].rearrange("p g r -> p (g r)"),
-                    in_=gt[:],
-                )
-                codes[unit] = cd
-                scales[unit] = sc
-                return
-            n, t = divmod(unit - 4, 4)
-            if t == 0:
-                codes[4 + n] = keep.tile([P, 4, 512], U32, name="wc%d" % n, align_bytes=64)
-                scales[4 + n] = keep.tile([P, 4, 512], U8, name="ws%d" % n, align_bytes=64)
-            cols = slice(t * P, (t + 1) * P)
-            for g in range(4):
-                nc.vector.quantize_mx(
-                    out=codes[4 + n][:, g, cols].bitcast(E5X4),
-                    scales=scales[4 + n][:, g, cols],
-                    in_=gt[:, g * 512 : (g + 1) * 512],
-                )
+            cd = keep.tile([P, 512], U32, name="cd%d" % unit, align_bytes=64)
+            sc = keep.tile([P, 512], U8, name="sc%d" % unit, align_bytes=64)
+            nc.vector.quantize_mx(out=cd[:].bitcast(E5X4), scales=sc[:], in_=gt[:])
+            codes[unit] = cd
+            scales[unit] = sc
 
         def mx(j):
             n, m = divmod(j, 4)
             acc = accs.tile([P, 512], F32, name="acc")
             for g in range(4):
+                cols = slice(g * P, (g + 1) * P)
                 nc.tensor.matmul_mx(
                     out=acc[:],
-                    lhsT=codes[m][:, g, :].bitcast(E5X4),
-                    lhsT_scale=scales[m][:, g, :],
-                    rhs=codes[4 + n][:, g, :].bitcast(E5X4),
-                    rhs_scale=scales[4 + n][:, g, :],
+                    lhsT=codes[m][:, cols].bitcast(E5X4),
+                    lhsT_scale=scales[m][:, cols],
+                    rhs=codes[4 + 4 * n + g][:].bitcast(E5X4),
+                    rhs_scale=scales[4 + 4 * n + g][:],
                     start=(g == 0),
                     stop=(g == 3),
                 )
@@ -175,60 +167,71 @@ def tile_attention_pa_kernel(tc, x, freqs_cis, wqkv, q_norm_w, k_norm_w, out_0, 
             pt = m % 2
             acc = acc_of[j]
             rs = rs_of[j]
-            t1 = outp.tile([P, 512], F32, name="t1")
-            t2 = work.tile([P, 512], F32, name="t2")
+            pp = work.tile([P, 4, 2, HD], F32, name="pp")
             for h in range(4):
-                sl = slice(h * HD, (h + 1) * HD)
                 nc.vector.scalar_tensor_tensor(
-                    out=t1[:, sl], in0=acc[:, sl], scalar=rs[:, h : h + 1], in1=tab[:, ws, pt, 0, :],
-                    op0=ALU.mult, op1=ALU.mult,
+                    out=pp[:, h, :, :],
+                    in0=acc[:, h * HD : (h + 1) * HD].unsqueeze(1).to_broadcast([P, 2, HD]),
+                    scalar=rs[:, h : h + 1],
+                    in1=tab[:, ws, pt, :, :],
+                    op0=ALU.mult,
+                    op1=ALU.mult,
                 )
-            for h in range(4):
-                sl = slice(h * HD, (h + 1) * HD)
-                nc.vector.scalar_tensor_tensor(
-                    out=pairs(t2[:, sl]), in0=pairs(acc[:, sl])[:, :, ::-1], scalar=rs[:, h : h + 1],
-                    in1=pairs(tab[:, ws, pt, 1, :]), op0=ALU.mult, op1=ALU.mult,
-                )
-            t1_of[j] = t1
-            t2_of[j] = t2
+            pp_of[j] = pp
 
-        def finish(j):
+        def combine(j):
+            pp = pp_of[j]
+            res = outp.tile([P, 512], F32, name="res")
+            nc.gpsimd.tensor_tensor(
+                out=res[:].rearrange("p (h j e) -> p h j e", h=4, e=2),
+                in0=pp[:, :, 0, :].rearrange("p h (j e) -> p h j e", e=2),
+                in1=pp[:, :, 1, :].rearrange("p h (j e) -> p h j e", e=2)[:, :, :, ::-1],
+                op=ALU.add,
+            )
+            out_of[j] = res
+
+        def plain_copy(j):
+            res = outp.tile([P, 512], F32, name="res")
+            if j % 2 == 0:
+                nc.scalar.copy(out=res[:], in_=acc_of[j][:])
+            else:
+                nc.vector.tensor_copy(out=res[:], in_=acc_of[j][:])
+            out_of[j] = res
+
+        def store(j):
             n, m = divmod(j, 4)
-            t1 = t1_of[j]
             rows = slice(m * P, (m + 1) * P)
-            if n < 5:
-                nc.gpsimd.tensor_tensor(out=t1[:], in0=t1[:], in1=t2_of[j][:], op=ALU.add)
             if n < 4:
                 dest = q_out[rows, n * 512 : (n + 1) * 512]
             elif n == 4:
                 dest = k_out[rows, :]
             else:
                 dest = v_out[rows, :]
-            nc.sync.dma_start(out=dest, in_=t1[:])
-
-        def plain_copy(j):
-            t1 = outp.tile([P, 512], F32, name="t1")
-            if j % 2 == 0:
-                nc.scalar.copy(out=t1[:], in_=acc_of[j][:])
-            else:
-                nc.vector.tensor_copy(out=t1[:], in_=acc_of[j][:])
-            t1_of[j] = t1
+            nc.sync.dma_start(out=dest, in_=out_of[j][:])
 
         for r in range(NRUN + 2):
-            for unit in (2 * r + AHEAD, 2 * r + AHEAD + 1):
-                if unit < 2 * NRUN:
-                    load(unit)
-            grouped = []
+            for i in (2 * r + AHEAD, 2 * r + AHEAD + 1):
+                if i < 2 * NRUN:
+                    load(i)
+            grouped = {}
             if r < NRUN:
-                for unit in (2 * r, 2 * r + 1):
-                    grouped.append((unit, transposes(unit)))
+                ua = 2 * r
+                ub = 2 * r + 1
+                grouped[ua] = grp.tile([P, 2048], BF16, name="grouped", align_bytes=64)
+                grouped[ub] = grp.tile([P, 2048], BF16, name="grouped", align_bytes=64)
+                if r < 2:
+                    order = [(ua, 0), (ua, 1), (ub, 0), (ub, 1)]
+                else:
+                    order = [(ua, 0), (ub, 0), (ua, 1), (ub, 1)]
+                for unit, b in order:
+                    transposes(unit, b, grouped[unit])
             if r == 1:
                 gains = spread_gains()
             banks = [2 * (r - LAG), 2 * (r - LAG) + 1] if r >= LAG else []
             for j in banks:
                 mx(j)
-            for unit, gt in grouped:
-                quantize(unit, gt)
+            for unit in sorted(grouped):
+                quantize(unit, grouped[unit])
             if r == 1:
                 tables(gains)
             for j in banks:
@@ -240,4 +243,6 @@ def tile_attention_pa_kernel(tc, x, freqs_cis, wqkv, q_norm_w, k_norm_w, out_0, 
                 if j < 20:
                     rotate(j)
             for j in banks:
-                finish(j)
+                if j < 20:
+                    combine(j)
+                store(j)

@@ -52,6 +52,7 @@ def tile_attention_pa_kernel(tc, x, freqs_cis, wqkv, q_norm_w, k_norm_w, out_0, 
         scales = {}
         acc_of = {}
         rs_of = {}
+        ss_of = {}
         pp_of = {}
         out_of = {}
 
@@ -151,14 +152,17 @@ def tile_attention_pa_kernel(tc, x, freqs_cis, wqkv, q_norm_w, k_norm_w, out_0, 
                 )
             acc_of[j] = acc
 
-        def stats(j):
+        def squares(j):
             acc = acc_of[j]
             ss = small.tile([P, 4], F32, name="ss")
             for h in range(4):
                 sl = slice(h * HD, (h + 1) * HD)
                 nc.scalar.activation(out=junk[:, sl], in_=acc[:, sl], func=ACT.Square, accum_out=ss[:, h : h + 1])
+            ss_of[j] = ss
+
+        def rsqrt(j):
             rs = small.tile([P, 4], F32, name="rs")
-            nc.scalar.activation(out=rs[:], in_=ss[:], func=ACT.Abs_reciprocal_sqrt, scale=1.0 / HD, bias=EPS)
+            nc.scalar.activation(out=rs[:], in_=ss_of[j][:], func=ACT.Abs_reciprocal_sqrt, scale=1.0 / HD, bias=EPS)
             rs_of[j] = rs
 
         def rotate(j):
@@ -209,40 +213,44 @@ def tile_attention_pa_kernel(tc, x, freqs_cis, wqkv, q_norm_w, k_norm_w, out_0, 
                 dest = v_out[rows, :]
             nc.sync.dma_start(out=dest, in_=out_of[j][:])
 
-        for r in range(NRUN + 2):
+        for r in range(NRUN + 3):
             for i in (2 * r + AHEAD, 2 * r + AHEAD + 1):
                 if i < 2 * NRUN:
                     load(i)
+            made = [2 * (r - LAG), 2 * (r - LAG) + 1] if LAG <= r < LAG + 12 else []
+            done = [2 * (r - 1 - LAG), 2 * (r - 1 - LAG) + 1] if LAG + 1 <= r else []
+            units = [2 * r, 2 * r + 1] if r < NRUN else []
             grouped = {}
-            if r < NRUN:
-                ua = 2 * r
-                ub = 2 * r + 1
-                grouped[ua] = grp.tile([P, 2048], BF16, name="grouped", align_bytes=64)
-                grouped[ub] = grp.tile([P, 2048], BF16, name="grouped", align_bytes=64)
-                if r < 2:
-                    order = [(ua, 0), (ua, 1), (ub, 0), (ub, 1)]
-                else:
-                    order = [(ua, 0), (ub, 0), (ua, 1), (ub, 1)]
-                for unit, b in order:
+            for unit in units:
+                grouped[unit] = grp.tile([P, 2048], BF16, name="grouped", align_bytes=64)
+            if units and not done and r >= 2:
+                for unit, b in [(units[0], 0), (units[1], 0), (units[0], 1), (units[1], 1)]:
                     transposes(unit, b, grouped[unit])
+                for unit in units:
+                    quantize(unit, grouped[unit])
+            else:
+                for half in range(2):
+                    e = done[half] if done else None
+                    normed = e is not None and e < 20
+                    if normed:
+                        squares(e)
+                    if units:
+                        transposes(units[half], 0, grouped[units[half]])
+                    if normed:
+                        rsqrt(e)
+                    if units:
+                        transposes(units[half], 1, grouped[units[half]])
+                    if normed:
+                        rotate(e)
+                    if units:
+                        quantize(units[half], grouped[units[half]])
+                    if normed:
+                        combine(e)
+                    if e is not None:
+                        if not normed:
+                            plain_copy(e)
+                        store(e)
             if r == 1:
-                gains = spread_gains()
-            banks = [2 * (r - LAG), 2 * (r - LAG) + 1] if r >= LAG else []
-            for j in banks:
+                tables(spread_gains())
+            for j in made:
                 mx(j)
-            for unit in sorted(grouped):
-                quantize(unit, grouped[unit])
-            if r == 1:
-                tables(gains)
-            for j in banks:
-                if j < 20:
-                    stats(j)
-                else:
-                    plain_copy(j)
-            for j in banks:
-                if j < 20:
-                    rotate(j)
-            for j in banks:
-                if j < 20:
-                    combine(j)
-                store(j)

@@ -59,7 +59,10 @@ def tile_attention_pa_kernel(tc, x, freqs_cis, wqkv, q_norm_w, k_norm_w, out_0, 
         def load(i):
             if i < 4:
                 raw = rawp.tile([P, D], BF16, name="raw")
-                nc.sync.dma_start(out=raw[:], in_=x_rows[i * P : (i + 1) * P, :])
+                pieces = 4 if i == 0 else 1
+                for c in range(pieces):
+                    cols = slice(c * D // pieces, (c + 1) * D // pieces)
+                    nc.sync.dma_start(out=raw[:, cols], in_=x_rows[i * P : (i + 1) * P, cols])
             else:
                 run, half = divmod(i - 4, 2)
                 n, kh = divmod(run, 2)
@@ -196,10 +199,7 @@ def tile_attention_pa_kernel(tc, x, freqs_cis, wqkv, q_norm_w, k_norm_w, out_0, 
 
         def plain_copy(j):
             res = outp.tile([P, 512], F32, name="res")
-            if j % 2 == 0:
-                nc.scalar.copy(out=res[:], in_=acc_of[j][:])
-            else:
-                nc.vector.tensor_copy(out=res[:], in_=acc_of[j][:])
+            nc.scalar.copy(out=res[:], in_=acc_of[j][:])
             out_of[j] = res
 
         def store(j):
@@ -211,7 +211,8 @@ def tile_attention_pa_kernel(tc, x, freqs_cis, wqkv, q_norm_w, k_norm_w, out_0, 
                 dest = k_out[rows, :]
             else:
                 dest = v_out[rows, :]
-            nc.sync.dma_start(out=dest, in_=out_of[j][:])
+            queue = nc.sync if n < 5 else nc.scalar
+            queue.dma_start(out=dest, in_=out_of[j][:])
 
         for r in range(NRUN + 3):
             for i in (2 * r + AHEAD, 2 * r + AHEAD + 1):

@@ -39,6 +39,7 @@ def tile_attention_pa_kernel(tc, x, freqs_cis, wqkv, q_norm_w, k_norm_w, out_0, 
         const = ctx.enter_context(tc.tile_pool(name="const", bufs=1))
         keep = ctx.enter_context(tc.tile_pool(name="keep", bufs=1))
         rawp = ctx.enter_context(tc.tile_pool(name="rawp", bufs=12))
+        sortp = ctx.enter_context(tc.tile_pool(name="sortp", bufs=4))
         grp = ctx.enter_context(tc.tile_pool(name="grp", bufs=4))
         small = ctx.enter_context(tc.tile_pool(name="small", bufs=4))
         work = ctx.enter_context(tc.tile_pool(name="work", bufs=4))
@@ -48,6 +49,7 @@ def tile_attention_pa_kernel(tc, x, freqs_cis, wqkv, q_norm_w, k_norm_w, out_0, 
         ctx.enter_context(tc.manual_schedule())
 
         raws = {}
+        sorted_of = {}
         codes = {}
         scales = {}
         acc_of = {}
@@ -74,12 +76,23 @@ def tile_attention_pa_kernel(tc, x, freqs_cis, wqkv, q_norm_w, k_norm_w, out_0, 
                 )
             raws[i] = raw
 
+        def sort_words(i):
+            raw = raws[i][:] if i < 4 else raws[i][:].rearrange("p t k -> p (t k)")
+            st = sortp.tile([P, 4, 2, P], F32, name="sorted")
+            nc.vector.tensor_copy(out=st[:], in_=raw.bitcast(F32).rearrange("p (q w u) -> p q u w", q=4, u=2))
+            sorted_of[i] = st
+
         def slab(unit, s, u):
             if unit < 4:
-                return raws[unit][:].bitcast(F32)[:, 256 * s + u : 256 * (s + 1) : 2]
-            gl = unit % 2
-            raw = raws[4 + 2 * (unit // 2 - 2) + s // 2]
-            return raw[:, s % 2, :].bitcast(F32)[:, 256 * gl + u : 256 * (gl + 1) : 2]
+                i = unit
+                q = s
+            else:
+                i = 4 + 2 * (unit // 2 - 2) + s // 2
+                q = 2 * (s % 2) + unit % 2
+            if i in sorted_of:
+                return sorted_of[i][:, q, u, :]
+            raw = raws[i][:] if i < 4 else raws[i][:].rearrange("p t k -> p (t k)")
+            return raw.bitcast(F32)[:, 256 * q + u : 256 * (q + 1) : 2]
 
         wrow = const.tile([P, 2 * HD], BF16, name="wrow")
         nc.gpsimd.memset(wrow[:], 0.0)
@@ -221,6 +234,8 @@ def tile_attention_pa_kernel(tc, x, freqs_cis, wqkv, q_norm_w, k_norm_w, out_0, 
             made = [2 * (r - LAG), 2 * (r - LAG) + 1] if LAG <= r < LAG + 12 else []
             done = [2 * (r - 1 - LAG), 2 * (r - 1 - LAG) + 1] if LAG + 1 <= r else []
             units = [2 * r, 2 * r + 1] if r < NRUN else []
+            if r <= LAG:
+                sort_words(2 * r + 1)
             grouped = {}
             for unit in units:
                 grouped[unit] = grp.tile([P, 2048], BF16, name="grouped", align_bytes=64)
@@ -253,5 +268,7 @@ def tile_attention_pa_kernel(tc, x, freqs_cis, wqkv, q_norm_w, k_norm_w, out_0, 
                         store(e)
             if r == 1:
                 tables(spread_gains())
+            if LAG <= r < NRUN - 1 and r % 2 == 0:
+                sort_words(2 * (r + 1) + 1)
             for j in made:
                 mx(j)

@@ -234,8 +234,6 @@ def tile_attention_pa_kernel(tc, x, freqs_cis, wqkv, q_norm_w, k_norm_w, out_0, 
             made = [2 * (r - LAG), 2 * (r - LAG) + 1] if LAG <= r < LAG + 12 else []
             done = [2 * (r - 1 - LAG), 2 * (r - 1 - LAG) + 1] if LAG + 1 <= r else []
             units = [2 * r, 2 * r + 1] if r < NRUN else []
-            if r <= LAG:
-                sort_words(2 * r + 1)
             grouped = {}
             for unit in units:
                 grouped[unit] = grp.tile([P, 2048], BF16, name="grouped", align_bytes=64)
@@ -268,7 +266,7 @@ def tile_attention_pa_kernel(tc, x, freqs_cis, wqkv, q_norm_w, k_norm_w, out_0, 
                         store(e)
             if r == 1:
                 tables(spread_gains())
-            if LAG <= r < NRUN - 1 and r % 2 == 0:
-                sort_words(2 * (r + 1) + 1)
+            if LAG < r + 2 < NRUN and r % 2 == 1:
+                sort_words(2 * (r + 2) + 1)
             for j in made:
                 mx(j)

@@ -266,7 +266,7 @@ def tile_attention_pa_kernel(tc, x, freqs_cis, wqkv, q_norm_w, k_norm_w, out_0, 
                         store(e)
             if r == 1:
                 tables(spread_gains())
-            if LAG < r + 2 < NRUN and r % 2 == 1:
+            if LAG < r + 2 < NRUN:
                 sort_words(2 * (r + 2) + 1)
             for j in made:
                 mx(j)

from contextlib import ExitStack

import concourse.mybir as mybir
from concourse.masks import make_identity

F32 = mybir.dt.float32
BF16 = mybir.dt.bfloat16
U32 = mybir.dt.uint32
U8 = mybir.dt.uint8
E5X4 = mybir.dt.float8_e5m2_x4
ACT = mybir.ActivationFunctionType
ALU = mybir.AluOpType

P = 128
TOKENS = 512
D = 2048
E = 3072
HD = 128
EPS = 1e-6
NRUN = 14
LAG = 4
AHEAD = 8

FLOPS = 2 * TOKENS * E * D


def pairs(ap):
    return ap.rearrange("p (j e) -> p j e", e=2)


def tile_attention_pa_kernel(tc, x, freqs_cis, wqkv, q_norm_w, k_norm_w, out_0, out_1, out_2):
    nc = tc.nc
    x_rows = x.rearrange("b s k -> (b s) k")
    q_out = out_0.rearrange("b s h d -> (b s) (h d)")
    k_out = out_1.rearrange("b s h d -> (b s) (h d)")
    v_out = out_2.rearrange("b s h d -> (b s) (h d)")

    with ExitStack() as ctx:
        const = ctx.enter_context(tc.tile_pool(name="const", bufs=1))
        keep = ctx.enter_context(tc.tile_pool(name="keep", bufs=1))
        rawp = ctx.enter_context(tc.tile_pool(name="rawp", bufs=12))
        sortp = ctx.enter_context(tc.tile_pool(name="sortp", bufs=4))
        grp = ctx.enter_context(tc.tile_pool(name="grp", bufs=4))
        small = ctx.enter_context(tc.tile_pool(name="small", bufs=4))
        work = ctx.enter_context(tc.tile_pool(name="work", bufs=4))
        outp = ctx.enter_context(tc.tile_pool(name="outp", bufs=8))
        tps = ctx.enter_context(tc.psum_pool(name="tps", bufs=4))
        accs = ctx.enter_context(tc.psum_pool(name="accs", bufs=4))
        ctx.enter_context(tc.manual_schedule())

        raws = {}
        sorted_of = {}
        codes = {}
        scales = {}
        acc_of = {}
        rs_of = {}
        ss_of = {}
        pp_of = {}
        out_of = {}

        def load(i):
            if i < 4:
                raw = rawp.tile([P, D], BF16, name="raw")
                pieces = 4 if i == 0 else 1
                for c in range(pieces):
                    cols = slice(c * D // pieces, (c + 1) * D // pieces)
                    nc.sync.dma_start(out=raw[:, cols], in_=x_rows[i * P : (i + 1) * P, cols])
            else:
                run, half = divmod(i - 4, 2)
                n, kh = divmod(run, 2)
                r0 = n * 512 + half * 256
                raw = rawp.tile([P, 2, 1024], BF16, name="raw")
                nc.sync.dma_start(
                    out=raw[:],
                    in_=wqkv[r0 : r0 + 256, kh * 1024 : (kh + 1) * 1024].rearrange("(t p) k -> p t k", p=P),
                )
            raws[i] = raw

        def sort_words(i):
            raw = raws[i][:] if i < 4 else raws[i][:].rearrange("p t k -> p (t k)")
            st = sortp.tile([P, 4, 2, P], F32, name="sorted")
            nc.vector.tensor_copy(out=st[:], in_=raw.bitcast(F32).rearrange("p (q w u) -> p q u w", q=4, u=2))
            sorted_of[i] = st

        def slab(unit, s, u):
            if unit < 4:
                i = unit
                q = s
            else:
                i = 4 + 2 * (unit // 2 - 2) + s // 2
                q = 2 * (s % 2) + unit % 2
            if i in sorted_of:
                return sorted_of[i][:, q, u, :]
            raw = raws[i][:] if i < 4 else raws[i][:].rearrange("p t k -> p (t k)")
            return raw.bitcast(F32)[:, 256 * q + u : 256 * (q + 1) : 2]

        wrow = const.tile([P, 2 * HD], BF16, name="wrow")
        nc.gpsimd.memset(wrow[:], 0.0)
        freqs = const.tile([P, 2, HD], BF16, name="freqs")
        nc.scalar.dma_start(out=freqs[:], in_=freqs_cis.rearrange("(t p) j e -> p t (j e)", p=P))
        nc.scalar.dma_start(out=wrow[0:1, 0:HD], in_=q_norm_w.rearrange("(o d) -> o d", o=1))
        nc.scalar.dma_start(out=wrow[0:1, HD : 2 * HD], in_=k_norm_w.rearrange("(o d) -> o d", o=1))
        for i in range(AHEAD):
            load(i)
        ident = const.tile([P, P], F32, name="ident")
        make_identity(nc, ident[:])
        ones = const.tile([P, P], BF16, name="ones")
        nc.gpsimd.memset(ones[:], 1.0)
        warm = const.tile([P, 1], F32, name="warm")
        nc.gpsimd.memset(warm[:], 1.0)
        warm2 = const.tile([P, 1], F32, name="warm2")
        nc.scalar.activation(out=warm2[:], in_=warm[:], func=ACT.Abs_reciprocal_sqrt)
        junk = const.tile([P, 4 * HD], F32, name="junk")
        tab = const.tile([P, 2, 2, 2, HD], F32, name="tab")

        def spread_gains():
            wb = accs.tile([P, 512], F32, name="acc")
            nc.tensor.matmul(out=wb[:, 0 : 2 * HD], lhsT=ones[:], rhs=wrow[:], start=True, stop=True)
            return wb

        def tables(wb):
            for ws in range(2):
                w3 = pairs(wb[:, ws * HD : (ws + 1) * HD])
                for pt in range(2):
                    f3 = pairs(freqs[:, pt, :])
                    c1 = pairs(tab[:, ws, pt, 0, :])
                    c2 = pairs(tab[:, ws, pt, 1, :])
                    for e in range(2):
                        nc.vector.tensor_tensor(
                            out=c1[:, :, e : e + 1], in0=w3[:, :, e : e + 1], in1=f3[:, :, 0:1], op=ALU.mult
                        )
                    nc.vector.tensor_tensor(out=c2[:, :, 0:1], in0=w3[:, :, 0:1], in1=f3[:, :, 1:2], op=ALU.mult)
                    nc.vector.scalar_tensor_tensor(
                        out=c2[:, :, 1:2], in0=w3[:, :, 1:2], scalar=-1.0, in1=f3[:, :, 1:2],
                        op0=ALU.mult, op1=ALU.mult,
                    )

        def transposes(unit, b, gt):
            tp = tps.tile([P, 2, 2, P], F32, name="tp")
            for sl in range(2):
                for u in range(2):
                    nc.tensor.transpose(tp[:, sl, u, :], slab(unit, 2 * b + sl, u), ident[:])
            nc.scalar.copy(
                out=gt[:].bitcast(F32)[:, 512 * b : 512 * (b + 1)].rearrange("p (s r u) -> p s r u", s=2, u=2),
                in_=tp[:].rearrange("p s u r -> p s r u"),
            )

        def quantize(unit, gt):
            cd = keep.tile([P, 512], U32, name="cd%d" % unit, align_bytes=64)
            sc = keep.tile([P, 512], U8, name="sc%d" % unit, align_bytes=64)
            nc.vector.quantize_mx(out=cd[:].bitcast(E5X4), scales=sc[:], in_=gt[:])
            codes[unit] = cd
            scales[unit] = sc

        def mx(j):
            n, m = divmod(j, 4)
            acc = accs.tile([P, 512], F32, name="acc")
            for g in range(4):
                cols = slice(g * P, (g + 1) * P)
                nc.tensor.matmul_mx(
                    out=acc[:],
                    lhsT=codes[m][:, cols].bitcast(E5X4),
                    lhsT_scale=scales[m][:, cols],
                    rhs=codes[4 + 4 * n + g][:].bitcast(E5X4),
                    rhs_scale=scales[4 + 4 * n + g][:],
                    start=(g == 0),
                    stop=(g == 3),
                )
            acc_of[j] = acc

        def squares(j):
            acc = acc_of[j]
            ss = small.tile([P, 4], F32, name="ss")
            for h in range(4):
                sl = slice(h * HD, (h + 1) * HD)
                nc.scalar.activation(out=junk[:, sl], in_=acc[:, sl], func=ACT.Square, accum_out=ss[:, h : h + 1])
            ss_of[j] = ss

        def rsqrt(j):
            rs = small.tile([P, 4], F32, name="rs")
            nc.scalar.activation(out=rs[:], in_=ss_of[j][:], func=ACT.Abs_reciprocal_sqrt, scale=1.0 / HD, bias=EPS)
            rs_of[j] = rs

        def rotate(j):
            n, m = divmod(j, 4)
            ws = 0 if n < 4 else 1
            pt = m % 2
            acc = acc_of[j]
            rs = rs_of[j]
            pp = work.tile([P, 4, 2, HD], F32, name="pp")
            for h in range(4):
                nc.vector.scalar_tensor_tensor(
                    out=pp[:, h, :, :],
                    in0=acc[:, h * HD : (h + 1) * HD].unsqueeze(1).to_broadcast([P, 2, HD]),
                    scalar=rs[:, h : h + 1],
                    in1=tab[:, ws, pt, :, :],
                    op0=ALU.mult,
                    op1=ALU.mult,
                )
            pp_of[j] = pp

        def combine(j):
            pp = pp_of[j]
            res = outp.tile([P, 512], F32, name="res")
            nc.gpsimd.tensor_tensor(
                out=res[:].rearrange("p (h j e) -> p h j e", h=4, e=2),
                in0=pp[:, :, 0, :].rearrange("p h (j e) -> p h j e", e=2),
                in1=pp[:, :, 1, :].rearrange("p h (j e) -> p h j e", e=2)[:, :, :, ::-1],
                op=ALU.add,
            )
            out_of[j] = res

        def plain_copy(j):
            res = outp.tile([P, 512], F32, name="res")
            nc.scalar.copy(out=res[:], in_=acc_of[j][:])
            out_of[j] = res

        def store(j):
            n, m = divmod(j, 4)
            rows = slice(m * P, (m + 1) * P)
            if n < 4:
                dest = q_out[rows, n * 512 : (n + 1) * 512]
            elif n == 4:
                dest = k_out[rows, :]
            else:
                dest = v_out[rows, :]
            queue = nc.sync if n < 5 else nc.scalar
            queue.dma_start(out=dest, in_=out_of[j][:])

        for r in range(NRUN + 3):
            for i in (2 * r + AHEAD, 2 * r + AHEAD + 1):
                if i < 2 * NRUN:
                    load(i)
            made = [2 * (r - LAG), 2 * (r - LAG) + 1] if LAG <= r < LAG + 12 else []
            done = [2 * (r - 1 - LAG), 2 * (r - 1 - LAG) + 1] if LAG + 1 <= r else []
            units = [2 * r, 2 * r + 1] if r < NRUN else []
            grouped = {}
            for unit in units:
                grouped[unit] = grp.tile([P, 2048], BF16, name="grouped", align_bytes=64)
            if units and not done and r >= 2:
                for unit, b in [(units[0], 0), (units[1], 0), (units[0], 1), (units[1], 1)]:
                    transposes(unit, b, grouped[unit])
                for unit in units:
                    quantize(unit, grouped[unit])
            else:
                for half in range(2):
                    e = done[half] if done else None
                    normed = e is not None and e < 20
                    if normed:
                        squares(e)
                    if units:
                        transposes(units[half], 0, grouped[units[half]])
                    if normed:
                        rsqrt(e)
                    if units:
                        transposes(units[half], 1, grouped[units[half]])
                    if normed:
                        rotate(e)
                    if units:
                        quantize(units[half], grouped[units[half]])
                    if normed:
                        combine(e)
                    if e is not None:
                        if not normed:
                            plain_copy(e)
                        store(e)
            if r == 1:
                tables(spread_gains())
            if LAG < r + 2 < NRUN:
                sort_words(2 * (r + 2) + 1)
            for j in made:
                mx(j)
